import numpy as np
import ml_dtypes


def mxq(x, axis, fmt="e4m3"):
    dtype, down = {"e4m3": (ml_dtypes.float8_e4m3fn, 7), "e5m2": (ml_dtypes.float8_e5m2, 14)}[fmt]
    v = np.moveaxis(np.asarray(x, np.float32).astype(ml_dtypes.bfloat16).astype(np.float64), axis, -1)
    blocks = v.reshape(v.shape[:-1] + (-1, 32))
    amax = np.abs(blocks).max(-1, keepdims=True)
    byte = np.maximum(np.where(amax > 0, np.frexp(amax)[1] - 1 + 127, 0) - down, 1)
    scale = np.exp2(byte - 127.0)
    codes = (blocks / scale).astype(np.float32).astype(dtype).astype(np.float64)
    return np.moveaxis((codes * scale).reshape(v.shape), -1, axis)


WIDE = False


def mx_kscale(k):
    if not WIDE:
        return np.ones(k)
    levels = np.array([10, -10, 5, -5, 0])
    if k % 512:
        return np.exp2(np.random.permutation(np.resize(levels, k // 32))).repeat(32)
    a = np.empty((k // 512, 16))
    for p in range(k // 512):
        a[p, :8] = np.random.permutation(np.resize(levels, 8))
        for g in range(8):
            far = levels[np.abs(levels - a[p, g]) >= 10]
            a[p, g + 8] = far[np.random.randint(len(far))]
    return np.exp2(a.ravel()).repeat(32)


BF16 = ml_dtypes.bfloat16


def bf(x):
    return np.asarray(x, np.float32).astype(BF16)


def f64(x):
    return np.asarray(x).astype(np.float64)


B, N, D, H, DH = 2, 512, 1024, 16, 64
INNER = H * DH
S = 2 * DH


def dpfp(u):
    u2 = np.concatenate([np.maximum(u, 0.0), np.maximum(-u, 0.0)], axis=-1)
    return u2 * np.roll(u2, 1, axis=-1)


def draw0():
    s, t = mx_kscale(D), mx_kscale(N)
    f = dpfp(np.random.standard_normal((B, H, N, DH)))
    return {"x": bf(np.random.standard_normal((B, N, D)) * s),
            "wv": bf(np.random.standard_normal((D, INNER)) / np.sqrt(D) / s[:, None]),
            "beta": bf(np.random.standard_normal((B, H, N)) * t),
            "vo": bf(np.random.standard_normal((B, H, N, DH)) * 0.3),
            "k_phi": bf(f / f.sum(-1, keepdims=True) / t[:, None]),
            "W": bf(np.random.standard_normal((B, H, S, DH)))}


def core(x, wv, beta, vo, k_phi, W):
    v = mxq(f64(x), 2, "e4m3") @ mxq(f64(wv), 0, "e4m3")
    v = v.reshape(B, N, H, DH).transpose(0, 2, 1, 3)
    dv = f64(beta)[..., None] * (v - f64(vo))
    return f64(W) + (mxq(f64(k_phi).transpose(0, 1, 3, 2), 3, "e4m3") @ mxq(dv, 2, "e4m3"))


def e4m3fn_bytes(y):
    return np.clip(np.asarray(y, np.float64), -448.0, 448.0).astype(np.float32).astype(ml_dtypes.float8_e4m3fn).view(np.uint8)


def e4m3fn_values(b):
    return np.asarray(b, np.uint8).view(ml_dtypes.float8_e4m3fn).astype(np.float64)


def setup_inputs():
    d = draw0()
    x0 = np.asarray(d['k_phi']).astype(np.float64)
    s = (np.max(np.abs(x0), axis=(0, 1, 3), keepdims=True) / 448.0).astype(np.float32)
    out = {}
    for k, v in d.items():
        if k == 'k_phi':
            out['k_phi_bytes'] = e4m3fn_bytes(x0 / s.astype(np.float64))
            out['k_phi_scale'] = s
        else:
            out[k] = v
    return out


def reference(x, wv, beta, vo, k_phi_bytes, k_phi_scale, W):
    return core(x, wv, beta, vo, e4m3fn_values(k_phi_bytes) * k_phi_scale.astype(np.float64), W)

@@ -1,0 +1,360 @@
+from contextlib import ExitStack
+
+import concourse.mybir as mybir
+from concourse.masks import make_identity
+
+B, N, D, H, DH = 2, 512, 1024, 16, 64
+S = 128
+FLOPS = 2 * B * N * D * H * DH + 2 * B * H * N * S * DH
+
+F32 = mybir.dt.float32
+BF16 = mybir.dt.bfloat16
+U32 = mybir.dt.uint32
+U8 = mybir.dt.uint8
+FP8 = mybir.dt.float8_e4m3fn
+FP8X4 = mybir.dt.float8_e4m3fn_x4
+MULT = mybir.AluOpType.mult
+ADD = mybir.AluOpType.add
+SUB = mybir.AluOpType.subtract
+COPY = mybir.ActivationFunctionType.Copy
+
+P = 128
+PACK = 4
+CH = 256
+NCH = H * DH // CH
+PAIRS = B * H // 2
+WIDEN_ON_V = (0, 1)
+COPY_ON_V = (0, 1, 2, 3)
+QUADS = PAIRS // 2
+
+
+def tile_dpfpattention_pb_kernel(tc, x, wv, beta, vo, k_bytes, k_scale, W, out):
+    nc = tc.nc
+    with ExitStack() as ctx:
+        keep = ctx.enter_context(tc.tile_pool(name="keep", bufs=1))
+        work = ctx.enter_context(tc.tile_pool(name="work", bufs=4))
+        psx = ctx.enter_context(tc.psum_pool(name="psx", bufs=2))
+        psv = ctx.enter_context(tc.psum_pool(name="psv", bufs=4))
+        pso = ctx.enter_context(tc.psum_pool(name="pso", bufs=2))
+
+        ident = keep.tile([P, P], F32, name="ident")
+        identb = keep.tile([P, P], BF16, name="identb")
+        brow = keep.tile([P, N], BF16, name="brow")
+        bsb = keep.tile([P, B * H, PACK], BF16, name="bsb")
+        ksc = keep.tile([P, PACK], F32, name="ksc")
+        xc = [[keep.tile([P, 2, 2 * P], U32, align_bytes=64, name="xc%d%d" % (b, u)) for u in range(2)] for b in range(B)]
+        xs = [[keep.tile([P, 2, 2 * P], U8, align_bytes=64, name="xs%d%d" % (b, u)) for u in range(2)] for b in range(B)]
+        wc = [keep.tile([P, 2, CH], U32, align_bytes=64, name="wc%d" % c) for c in range(NCH)]
+        ws = [keep.tile([P, 2, CH], U8, align_bytes=64, name="ws%d" % c) for c in range(NCH)]
+        kc = [keep.tile([P, 4 * S], U32, align_bytes=64, name="kc%d" % i) for i in range(QUADS)]
+        ks = [keep.tile([P, 4 * S], U8, align_bytes=64, name="ks%d" % i) for i in range(QUADS)]
+        dc = [keep.tile([P, 4 * DH], U32, align_bytes=64, name="dc%d" % i) for i in range(QUADS)]
+        ds = [keep.tile([P, 4 * DH], U8, align_bytes=64, name="ds%d" % i) for i in range(QUADS)]
+        kb = [keep.tile([P, 4, PACK * S], U8, name="kb%d" % q) for q in range(8)]
+        vs = [keep.tile([P, 4, PACK, DH], BF16, name="vs%d" % q) for q in range(8)]
+        wt = [keep.tile([P, 8, DH], BF16, name="wt%d" % q) for q in range(4)]
+        ot = [keep.tile([P, 8, DH], F32, name="ot%d" % q) for q in range(4)]
+        xr = [[keep.tile([P, 2, D], BF16, name="xr%d%d" % (b, u)) for u in range(2)] for b in range(B)]
+        wr = [[keep.tile([P, PACK, CH], BF16, name="wr%d%d" % (c, g)) for g in range(2)] for c in range(NCH)]
+
+        make_identity(nc, ident[:])
+        nc.gpsimd.memset(brow[:], 0.0)
+        make_identity(nc, identb[:])
+
+        def load_k(q):
+            b, h0 = q // 4, 4 * (q % 4)
+            nc.sync.dma_start(
+                out=kb[q][:],
+                in_=k_bytes[b, h0 : h0 + 4].rearrange("h (p t) s -> p h (t s)", t=PACK),
+            )
+
+        def load_vo(q):
+            b, h0 = q // 4, 4 * (q % 4)
+            nc.sync.dma_start(
+                out=vs[q][:].rearrange("p h t d -> p h (t d)"),
+                in_=vo[b, h0 : h0 + 4].rearrange("h (p t) d -> p h (t d)", t=PACK),
+            )
+
+        def load_x(b, h):
+            nc.sync.dma_start(
+                out=xr[b][h][:],
+                in_=x[b].rearrange("(m t) k -> m t k", t=PACK)[:, 2 * h : 2 * h + 2, :],
+            )
+
+        def load_wv(c):
+            for g in range(2):
+                nc.sync.dma_start(
+                    out=wr[c][g][:],
+                    in_=wv.rearrange("(g p j) w -> g p j w", g=2, j=PACK)[g][:, :, CH * c : CH * (c + 1)],
+                )
+
+        def load_w(q):
+            b, h0 = q // 2, 8 * (q % 2)
+            nc.sync.dma_start(out=wt[q][:], in_=W[b, h0 : h0 + 8].rearrange("h s d -> s h d"))
+
+        nc.sync.dma_start(out=ksc[:], in_=k_scale.rearrange("a c (p t) e -> p (a c t e)", t=PACK))
+        load_k(0)
+        load_k(1)
+        load_x(0, 0)
+        load_x(0, 1)
+        load_wv(0)
+        load_k(2)
+        nc.sync.dma_start(out=brow[0 : B * H, :], in_=beta.rearrange("b h n -> (b h) n"))
+        load_vo(0)
+        load_wv(1)
+        load_k(3)
+        load_vo(1)
+        load_wv(2)
+        load_x(1, 0)
+        load_x(1, 1)
+        load_vo(2)
+        load_k(4)
+        load_wv(3)
+        load_vo(3)
+        load_k(5)
+        load_w(0)
+        load_vo(4)
+        load_k(6)
+        load_vo(5)
+        load_k(7)
+        load_w(1)
+        load_vo(6)
+        load_vo(7)
+        load_w(2)
+        load_w(3)
+
+        kw_t = {}
+        kg_t = {}
+
+        def widen(i):
+            kw = work.tile([P, 2, PACK, S], BF16, name="kw")
+            kw_t[i] = kw
+            for h in range(2):
+                src = kb[i // 2]
+                for t in range(PACK):
+                    sv = src[:, 2 * (i % 2) + h, S * t : S * (t + 1)].bitcast(FP8)
+                    if i in WIDEN_ON_V:
+                        nc.vector.tensor_scalar(
+                            out=kw[:, h, t, :], in0=sv, scalar1=ksc[:, t : t + 1], scalar2=None, op0=MULT
+                        )
+                    else:
+                        nc.scalar.activation(out=kw[:, h, t, :], in_=sv, func=COPY, scale=ksc[:, t : t + 1])
+
+        def kcopy(i):
+            if i % 2 == 0:
+                kg_t[i // 2] = work.tile([P, 4, S, PACK], BF16, align_bytes=64, name="kg")
+            dst = kg_t[i // 2][:, 2 * (i % 2) : 2 * (i % 2) + 2]
+            src = kw_t[i][:].rearrange("p h t s -> p h s t")
+            if i in COPY_ON_V:
+                nc.vector.tensor_copy(out=dst, in_=src)
+            else:
+                nc.scalar.copy(out=dst, in_=src)
+
+        def kquant(q, a=0, e=4):
+            nc.vector.quantize_mx(
+                out=kc[q][:, S * a : S * e].bitcast(FP8X4),
+                scales=ks[q][:, S * a : S * e],
+                in_=kg_t[q][:, a:e].rearrange("p h s t -> p (h s t)"),
+            )
+
+        xg_t = {}
+        xt_t = {}
+
+        def xtrans(b, h, g):
+            xt = psx.tile([P, 2, 2, P], F32, name="xt")
+            xt_t[(b, h, g)] = xt
+            for tt in range(2):
+                words = xr[b][h][:, tt, 512 * g : 512 * (g + 1)].bitcast(F32)
+                for u in range(2):
+                    nc.tensor.transpose(xt[:, tt, u, :], words[:, u::2], ident[:])
+
+        def xcopy(b, h, g):
+            if g == 0:
+                xg_t[(b, h)] = work.tile([P, N * PACK], BF16, align_bytes=64, name="xg", bufs=2)
+            nc.scalar.copy(
+                out=xg_t[(b, h)][:, 1024 * g : 1024 * (g + 1)]
+                .bitcast(F32)
+                .rearrange("p (t m u) -> p t m u", t=2, u=2),
+                in_=xt_t[(b, h, g)][:].rearrange("p t u m -> p t m u"),
+            )
+
+        def xquant(b, h):
+            nc.vector.quantize_mx(
+                out=xc[b][h][:].rearrange("p g n -> p (g n)").bitcast(FP8X4),
+                scales=xs[b][h][:].rearrange("p g n -> p (g n)"),
+                in_=xg_t[(b, h)][:],
+            )
+
+        wg_t = {}
+
+        def wcopy(c, g):
+            if c not in wg_t:
+                wg_t[c] = work.tile([P, 2, CH, PACK], BF16, align_bytes=64, name="wg", bufs=2)
+            src = wr[c][g][:].rearrange("p j w -> p w j")
+            nc.vector.tensor_copy(out=wg_t[c][:, g], in_=src)
+
+        def wquant(c):
+            nc.vector.quantize_mx(
+                out=wc[c][:].rearrange("p g w -> p (g w)").bitcast(FP8X4),
+                scales=ws[c][:].rearrange("p g w -> p (g w)"),
+                in_=wg_t[c][:].rearrange("p g w j -> p (g w j)"),
+            )
+
+        v_t = {}
+
+        def mm1(i):
+            b, j = i // 8, i % 8
+            c, o = j // 2, 128 * (j % 2)
+            v = psv.tile([P, PACK, P], F32, name="v")
+            v_t[i] = v
+            for t in range(PACK):
+                for g in range(2):
+                    nc.tensor.matmul_mx(
+                        out=v[:, t, :],
+                        lhsT=xc[b][t // 2][:, g, P * (t % 2) : P * (t % 2 + 1)].bitcast(FP8X4),
+                        lhsT_scale=xs[b][t // 2][:, g, P * (t % 2) : P * (t % 2 + 1)],
+                        rhs=wc[c][:, g, o : o + P].bitcast(FP8X4),
+                        rhs_scale=ws[c][:, g, o : o + P],
+                        start=(g == 0),
+                        stop=(g == 1),
+                    )
+
+        tm_t = {}
+        dg_t = {}
+
+        def pass1(i):
+            if i % 2 == 0:
+                tm_t[i // 2] = work.tile([P, 4, DH, PACK], F32, name="tm", bufs=3)
+            h0 = 2 * (i % 2)
+            nc.vector.tensor_tensor(
+                out=tm_t[i // 2][:, h0 : h0 + 2],
+                in0=v_t[i][:].rearrange("p t (h d) -> p h d t", h=2),
+                in1=vs[i // 2][:, h0 : h0 + 2].rearrange("p h t d -> p h d t"),
+                op=SUB,
+            )
+
+        def pass2(q, a=0, e=4):
+            if a == 0:
+                dg_t[q] = work.tile([P, 4, DH, PACK], BF16, align_bytes=64, name="dg", bufs=3)
+            nc.vector.tensor_tensor(
+                out=dg_t[q][:, a:e],
+                in0=tm_t[q][:, a:e],
+                in1=bsb[:, 4 * q + a : 4 * q + e, :].unsqueeze(2).to_broadcast([P, e - a, DH, PACK]),
+                op=MULT,
+            )
+
+        def dquant(q, a=0, e=4):
+            nc.vector.quantize_mx(
+                out=dc[q][:, DH * a : DH * e].bitcast(FP8X4),
+                scales=ds[q][:, DH * a : DH * e],
+                in_=dg_t[q][:, a:e].rearrange("p h d t -> p (h d t)"),
+            )
+
+        o_t = {}
+
+        def mm2(q, a=0, e=4):
+            if q % 2 == 0 and a == 0:
+                o_t[q // 2] = pso.tile([P, 8, DH], F32, name="o")
+            for h in range(a, e):
+                nc.tensor.matmul_mx(
+                    out=o_t[q // 2][:, 4 * (q % 2) + h, :],
+                    lhsT=kc[q][:, S * h : S * (h + 1)].bitcast(FP8X4),
+                    lhsT_scale=ks[q][:, S * h : S * (h + 1)],
+                    rhs=dc[q][:, DH * h : DH * (h + 1)].bitcast(FP8X4),
+                    rhs_scale=ds[q][:, DH * h : DH * (h + 1)],
+                    start=True,
+                    stop=True,
+                )
+
+        def finish(q, a, e):
+            nc.vector.tensor_tensor(out=ot[q][:, a:e, :], in0=o_t[q][:, a:e, :], in1=wt[q][:, a:e, :], op=ADD)
+            b, h0 = q // 2, 8 * (q % 2)
+            nc.sync.dma_start(
+                out=out[b, h0 + a : h0 + e].rearrange("h s d -> s h d"), in_=ot[q][:, a:e, :]
+            )
+
+        ctx.enter_context(tc.manual_schedule())
+        widen(0)
+        widen(2)
+        kcopy(0)
+        widen(1)
+        widen(3)
+        xtrans(0, 0, 0)
+        xtrans(0, 0, 1)
+        xcopy(0, 0, 0)
+        xtrans(0, 1, 0)
+        xcopy(0, 0, 1)
+        xtrans(0, 1, 1)
+        kcopy(1)
+        xcopy(0, 1, 0)
+        kcopy(2)
+        kquant(0)
+        kcopy(3)
+        xcopy(0, 1, 1)
+        xquant(0, 0)
+        kquant(1)
+        bt = psx.tile([P, PACK, P], BF16, name="xt")
+        for t in range(PACK):
+            nc.tensor.transpose(bt[:, t, :], brow[:, t::PACK], identb[:])
+        wcopy(0, 0)
+        xquant(0, 1)
+        wcopy(0, 1)
+        widen(4)
+        widen(5)
+        kcopy(4)
+        kcopy(5)
+        wcopy(1, 0)
+        wquant(0)
+        nc.vector.tensor_copy(out=bsb[:], in_=bt[:, :, 0 : B * H].rearrange("p t q -> p q t"))
+        mm1(0)
+        mm1(1)
+        wcopy(1, 1)
+        for q in range(QUADS):
+            last = q == QUADS - 1
+            if q in (1, 2):
+                xcopy(1, q - 1, 0)
+                xcopy(1, q - 1, 1)
+            for i in (2 * q + 6, 2 * q + 7):
+                if i < PAIRS:
+                    widen(i)
+            for i in (2 * q + 6, 2 * q + 7):
+                if i < PAIRS:
+                    kcopy(i)
+            pass1(2 * q)
+            if q + 1 < NCH:
+                wquant(q + 1)
+            if q == 3:
+                xquant(1, 1)
+            if not last:
+                mm1(2 * q + 2)
+            pass1(2 * q + 1)
+            if not last:
+                mm1(2 * q + 3)
+            if q in (0, 1):
+                xtrans(1, q, 0)
+                xtrans(1, q, 1)
+            if 1 <= q < QUADS - 2:
+                kquant(q + 1)
+            if q % 2 == 0 and q > 0:
+                finish(q // 2 - 1, 0, 8)
+            if last:
+                pass2(q, 0, 2)
+                kquant(q)
+                pass2(q, 2, 4)
+                finish(3, 0, 4)
+                dquant(q, 0, 2)
+                dquant(q, 2, 4)
+                mm2(q, 0, 2)
+                mm2(q, 2, 4)
+                finish(3, 4, 6)
+                finish(3, 6, 8)
+            else:
+                pass2(q)
+                if q + 2 < NCH:
+                    wcopy(q + 2, 0)
+                if q == 2:
+                    xquant(1, 0)
+                dquant(q)
+                if q + 2 < NCH:
+                    wcopy(q + 2, 1)
+                mm2(q)

@@ -20,11 +20,15 @@ COPY = mybir.ActivationFunctionType.Copy
 
 P = 128
 PACK = 4
-CH = 256
-NCH = H * DH // CH
+CHUNKS = ((0, 256), (256, 256), (512, 512))
+NCH = len(CHUNKS)
+C_OF = (0, 0, 1, 1, 2, 2, 2, 2)
 PAIRS = B * H // 2
-WIDEN_ON_V = (0, 1)
+WIDEN_ON_V = (0,)
 COPY_ON_V = (0, 1, 2, 3)
+COPY_BY_PE = ()
+WCOPY_ON_S = ()
+XCOPY_ON_V = ()
 QUADS = PAIRS // 2
 
 
@@ -34,18 +38,19 @@ def tile_dpfpattention_pb_kernel(tc, x, wv, beta, vo, k_bytes, k_scale, W, out):
         keep = ctx.enter_context(tc.tile_pool(name="keep", bufs=1))
         work = ctx.enter_context(tc.tile_pool(name="work", bufs=4))
         psx = ctx.enter_context(tc.psum_pool(name="psx", bufs=2))
-        psv = ctx.enter_context(tc.psum_pool(name="psv", bufs=4))
-        pso = ctx.enter_context(tc.psum_pool(name="pso", bufs=2))
+        psv = ctx.enter_context(tc.psum_pool(name="psv", bufs=3))
+        pso = ctx.enter_context(tc.psum_pool(name="pso", bufs=1))
+        psb = ctx.enter_context(tc.psum_pool(name="psb", bufs=1))
 
         ident = keep.tile([P, P], F32, name="ident")
         identb = keep.tile([P, P], BF16, name="identb")
         brow = keep.tile([P, N], BF16, name="brow")
-        bsb = keep.tile([P, B * H, PACK], BF16, name="bsb")
+        pick = keep.tile([P, B * H, 16], BF16, name="pick")
         ksc = keep.tile([P, PACK], F32, name="ksc")
         xc = [[keep.tile([P, 2, 2 * P], U32, align_bytes=64, name="xc%d%d" % (b, u)) for u in range(2)] for b in range(B)]
         xs = [[keep.tile([P, 2, 2 * P], U8, align_bytes=64, name="xs%d%d" % (b, u)) for u in range(2)] for b in range(B)]
-        wc = [keep.tile([P, 2, CH], U32, align_bytes=64, name="wc%d" % c) for c in range(NCH)]
-        ws = [keep.tile([P, 2, CH], U8, align_bytes=64, name="ws%d" % c) for c in range(NCH)]
+        wc = [keep.tile([P, 2, n], U32, align_bytes=64, name="wc%d" % c0) for c0, n in CHUNKS]
+        ws = [keep.tile([P, 2, n], U8, align_bytes=64, name="ws%d" % c0) for c0, n in CHUNKS]
         kc = [keep.tile([P, 4 * S], U32, align_bytes=64, name="kc%d" % i) for i in range(QUADS)]
         ks = [keep.tile([P, 4 * S], U8, align_bytes=64, name="ks%d" % i) for i in range(QUADS)]
         dc = [keep.tile([P, 4 * DH], U32, align_bytes=64, name="dc%d" % i) for i in range(QUADS)]
@@ -55,11 +60,14 @@ def tile_dpfpattention_pb_kernel(tc, x, wv, beta, vo, k_bytes, k_scale, W, out):
         wt = [keep.tile([P, 8, DH], BF16, name="wt%d" % q) for q in range(4)]
         ot = [keep.tile([P, 8, DH], F32, name="ot%d" % q) for q in range(4)]
         xr = [[keep.tile([P, 2, D], BF16, name="xr%d%d" % (b, u)) for u in range(2)] for b in range(B)]
-        wr = [[keep.tile([P, PACK, CH], BF16, name="wr%d%d" % (c, g)) for g in range(2)] for c in range(NCH)]
+        wr = [keep.tile([P, 2, PACK, n], BF16, name="wr%d" % c0) for c0, n in CHUNKS]
+        wg = [keep.tile([P, 2, n, PACK], BF16, align_bytes=64, name="wg%d" % c0) for c0, n in CHUNKS]
+        bp = [psb.tile([P, PACK, H * 16], BF16, name="bp%d" % b) for b in range(B)]
 
-        make_identity(nc, ident[:])
-        nc.gpsimd.memset(brow[:], 0.0)
         make_identity(nc, identb[:])
+        nc.gpsimd.memset(brow[:], 0.0)
+        make_identity(nc, ident[:])
+        nc.vector.tensor_copy(out=pick[:], in_=identb[:, 0 : B * H].unsqueeze(2).to_broadcast([P, B * H, 16]))
 
         def load_k(q):
             b, h0 = q // 4, 4 * (q % 4)
@@ -82,10 +90,11 @@ def tile_dpfpattention_pb_kernel(tc, x, wv, beta, vo, k_bytes, k_scale, W, out):
             )
 
         def load_wv(c):
+            c0, n = CHUNKS[c]
             for g in range(2):
                 nc.sync.dma_start(
-                    out=wr[c][g][:],
-                    in_=wv.rearrange("(g p j) w -> g p j w", g=2, j=PACK)[g][:, :, CH * c : CH * (c + 1)],
+                    out=wr[c][:, g],
+                    in_=wv.rearrange("(g p j) w -> g p j w", g=2, j=PACK)[g][:, :, c0 : c0 + n],
                 )
 
         def load_w(q):
@@ -98,25 +107,24 @@ def tile_dpfpattention_pb_kernel(tc, x, wv, beta, vo, k_bytes, k_scale, W, out):
         load_x(0, 0)
         load_x(0, 1)
         load_wv(0)
-        load_k(2)
         nc.sync.dma_start(out=brow[0 : B * H, :], in_=beta.rearrange("b h n -> (b h) n"))
+        load_k(2)
         load_vo(0)
         load_wv(1)
-        load_k(3)
         load_vo(1)
+        load_k(3)
         load_wv(2)
-        load_x(1, 0)
-        load_x(1, 1)
-        load_vo(2)
         load_k(4)
-        load_wv(3)
-        load_vo(3)
+        load_vo(2)
+        load_x(1, 0)
         load_k(5)
+        load_x(1, 1)
+        load_vo(3)
+        load_k(6)
         load_w(0)
         load_vo(4)
-        load_k(6)
-        load_vo(5)
         load_k(7)
+        load_vo(5)
         load_w(1)
         load_vo(6)
         load_vo(7)
@@ -127,7 +135,7 @@ def tile_dpfpattention_pb_kernel(tc, x, wv, beta, vo, k_bytes, k_scale, W, out):
         kg_t = {}
 
         def widen(i):
-            kw = work.tile([P, 2, PACK, S], BF16, name="kw")
+            kw = work.tile([P, 2, PACK, S], BF16, name="kw", bufs=8)
             kw_t[i] = kw
             for h in range(2):
                 src = kb[i // 2]
@@ -141,14 +149,28 @@ def tile_dpfpattention_pb_kernel(tc, x, wv, beta, vo, k_bytes, k_scale, W, out):
                         nc.scalar.activation(out=kw[:, h, t, :], in_=sv, func=COPY, scale=ksc[:, t : t + 1])
 
         def kcopy(i):
-            if i % 2 == 0:
-                kg_t[i // 2] = work.tile([P, 4, S, PACK], BF16, align_bytes=64, name="kg")
+            if i // 2 not in kg_t:
+                kg_t[i // 2] = work.tile([P, 4, S, PACK], BF16, align_bytes=64, name="kg", bufs=6)
             dst = kg_t[i // 2][:, 2 * (i % 2) : 2 * (i % 2) + 2]
-            src = kw_t[i][:].rearrange("p h t s -> p h s t")
+            if i in COPY_BY_PE:
+                nc.scalar.copy(out=dst, in_=kp_t[i][:])
+                return
+            dst = dst.rearrange("p h (c i) t -> p h c t i", i=4)
+            src = kw_t[i][:].rearrange("p h t (c i) -> p h c t i", i=4)
             if i in COPY_ON_V:
                 nc.vector.tensor_copy(out=dst, in_=src)
             else:
                 nc.scalar.copy(out=dst, in_=src)
+
+        kp_t = {}
+
+        def kturn(i):
+            kp = psx.tile([P, 2, S, PACK], BF16, name="xt")
+            kp_t[i] = kp
+            for h in range(2):
+                nc.tensor.matmul(
+                    kp[:, h], lhsT=identb[:], rhs=kw_t[i][:, h].rearrange("p t s -> p s t"), start=True, stop=True
+                )
 
         def kquant(q, a=0, e=4):
             nc.vector.quantize_mx(
@@ -171,7 +193,8 @@ def tile_dpfpattention_pb_kernel(tc, x, wv, beta, vo, k_bytes, k_scale, W, out):
         def xcopy(b, h, g):
             if g == 0:
                 xg_t[(b, h)] = work.tile([P, N * PACK], BF16, align_bytes=64, name="xg", bufs=2)
-            nc.scalar.copy(
+            copy = nc.vector.tensor_copy if (b, h, g) in XCOPY_ON_V else nc.scalar.copy
+            copy(
                 out=xg_t[(b, h)][:, 1024 * g : 1024 * (g + 1)]
                 .bitcast(F32)
                 .rearrange("p (t m u) -> p t m u", t=2, u=2),
@@ -185,26 +208,27 @@ def tile_dpfpattention_pb_kernel(tc, x, wv, beta, vo, k_bytes, k_scale, W, out):
                 in_=xg_t[(b, h)][:],
             )
 
-        wg_t = {}
-
         def wcopy(c, g):
-            if c not in wg_t:
-                wg_t[c] = work.tile([P, 2, CH, PACK], BF16, align_bytes=64, name="wg", bufs=2)
-            src = wr[c][g][:].rearrange("p j w -> p w j")
-            nc.vector.tensor_copy(out=wg_t[c][:, g], in_=src)
+            dst = wg[c][:, g].rearrange("p (c i) j -> p c j i", i=4)
+            src = wr[c][:, g].rearrange("p j (c i) -> p c j i", i=4)
+            if (c, g) in WCOPY_ON_S:
+                nc.scalar.copy(out=dst, in_=src)
+            else:
+                nc.vector.tensor_copy(out=dst, in_=src)
 
         def wquant(c):
             nc.vector.quantize_mx(
                 out=wc[c][:].rearrange("p g w -> p (g w)").bitcast(FP8X4),
                 scales=ws[c][:].rearrange("p g w -> p (g w)"),
-                in_=wg_t[c][:].rearrange("p g w j -> p (g w j)"),
+                in_=wg[c][:].rearrange("p g w j -> p (g w j)"),
             )
 
         v_t = {}
 
         def mm1(i):
             b, j = i // 8, i % 8
-            c, o = j // 2, 128 * (j % 2)
+            c = C_OF[j]
+            o = 128 * j - CHUNKS[c][0]
             v = psv.tile([P, PACK, P], F32, name="v")
             v_t[i] = v
             for t in range(PACK):
@@ -224,22 +248,26 @@ def tile_dpfpattention_pb_kernel(tc, x, wv, beta, vo, k_bytes, k_scale, W, out):
 
         def pass1(i):
             if i % 2 == 0:
-                tm_t[i // 2] = work.tile([P, 4, DH, PACK], F32, name="tm", bufs=3)
+                tm_t[i // 2] = work.tile([P, PACK, 4 * DH], F32, name="tm", bufs=4)
             h0 = 2 * (i % 2)
             nc.vector.tensor_tensor(
-                out=tm_t[i // 2][:, h0 : h0 + 2],
-                in0=v_t[i][:].rearrange("p t (h d) -> p h d t", h=2),
-                in1=vs[i // 2][:, h0 : h0 + 2].rearrange("p h t d -> p h d t"),
+                out=tm_t[i // 2][:, :, DH * h0 : DH * (h0 + 2)].rearrange("p t (h d) -> p t h d", h=2),
+                in0=v_t[i][:].rearrange("p t (h d) -> p t h d", h=2),
+                in1=vs[i // 2][:, h0 : h0 + 2].rearrange("p h t d -> p t h d"),
                 op=SUB,
             )
 
         def pass2(q, a=0, e=4):
             if a == 0:
-                dg_t[q] = work.tile([P, 4, DH, PACK], BF16, align_bytes=64, name="dg", bufs=3)
+                dg_t[q] = work.tile([P, 4, DH, PACK], BF16, align_bytes=64, name="dg", bufs=4)
+            n = (e - a) * 16
             nc.vector.tensor_tensor(
-                out=dg_t[q][:, a:e],
-                in0=tm_t[q][:, a:e],
-                in1=bsb[:, 4 * q + a : 4 * q + e, :].unsqueeze(2).to_broadcast([P, e - a, DH, PACK]),
+                out=dg_t[q][:, a:e].rearrange("p h (c i) t -> p (h c) t i", i=4),
+                in0=tm_t[q][:, :, DH * a : DH * e].rearrange("p t (c i) -> p c t i", i=4),
+                in1=bp[q // 4][:, :, 16 * (4 * (q % 4) + a) : 16 * (4 * (q % 4) + e)]
+                .rearrange("p t c -> p c t")
+                .unsqueeze(3)
+                .to_broadcast([P, n, PACK, 4]),
                 op=MULT,
             )
 
@@ -273,68 +301,81 @@ def tile_dpfpattention_pb_kernel(tc, x, wv, beta, vo, k_bytes, k_scale, W, out):
                 out=out[b, h0 + a : h0 + e].rearrange("h s d -> s h d"), in_=ot[q][:, a:e, :]
             )
 
-        ctx.enter_context(tc.manual_schedule())
+        def bload(b):
+            for t in range(PACK):
+                nc.tensor.matmul(
+                    bp[b][:, t],
+                    lhsT=brow[:, t::PACK],
+                    rhs=pick[:, H * b : H * (b + 1)].rearrange("p h c -> p (h c)"),
+                    start=True,
+                    stop=True,
+                )
+
         widen(0)
-        widen(2)
-        kcopy(0)
         widen(1)
+        kcopy(0)
+        widen(2)
+        kcopy(1)
         widen(3)
+        kquant(0)
+        kcopy(2)
+        kcopy(3)
         xtrans(0, 0, 0)
         xtrans(0, 0, 1)
         xcopy(0, 0, 0)
-        xtrans(0, 1, 0)
         xcopy(0, 0, 1)
-        xtrans(0, 1, 1)
-        kcopy(1)
-        xcopy(0, 1, 0)
-        kcopy(2)
-        kquant(0)
-        kcopy(3)
-        xcopy(0, 1, 1)
-        xquant(0, 0)
         kquant(1)
-        bt = psx.tile([P, PACK, P], BF16, name="xt")
-        for t in range(PACK):
-            nc.tensor.transpose(bt[:, t, :], brow[:, t::PACK], identb[:])
         wcopy(0, 0)
-        xquant(0, 1)
+        xtrans(0, 1, 0)
+        xtrans(0, 1, 1)
+        xcopy(0, 1, 0)
+        xcopy(0, 1, 1)
         wcopy(0, 1)
-        widen(4)
-        widen(5)
-        kcopy(4)
-        kcopy(5)
-        wcopy(1, 0)
+        xquant(0, 0)
         wquant(0)
-        nc.vector.tensor_copy(out=bsb[:], in_=bt[:, :, 0 : B * H].rearrange("p t q -> p q t"))
+        bload(0)
+        xquant(0, 1)
         mm1(0)
         mm1(1)
+        widen(4)
+        wcopy(1, 0)
+        widen(5)
         wcopy(1, 1)
         for q in range(QUADS):
             last = q == QUADS - 1
-            if q in (1, 2):
-                xcopy(1, q - 1, 0)
-                xcopy(1, q - 1, 1)
-            for i in (2 * q + 6, 2 * q + 7):
-                if i < PAIRS:
-                    widen(i)
-            for i in (2 * q + 6, 2 * q + 7):
-                if i < PAIRS:
+            if q == 2:
+                bload(1)
+                xcopy(1, 0, 0)
+                xcopy(1, 0, 1)
+            for i in (2 * q + 4, 2 * q + 5):
+                if i in COPY_BY_PE:
+                    kturn(i)
+                if i + 2 < PAIRS:
+                    widen(i + 2)
+                if i < PAIRS and i not in COPY_ON_V:
                     kcopy(i)
             pass1(2 * q)
-            if q + 1 < NCH:
-                wquant(q + 1)
+            if q == 0:
+                wquant(1)
+                wcopy(2, 0)
             if q == 3:
                 xquant(1, 1)
             if not last:
                 mm1(2 * q + 2)
             pass1(2 * q + 1)
+            if q == 0:
+                wcopy(2, 1)
             if not last:
                 mm1(2 * q + 3)
-            if q in (0, 1):
-                xtrans(1, q, 0)
-                xtrans(1, q, 1)
-            if 1 <= q < QUADS - 2:
-                kquant(q + 1)
+            if q in (1, 2):
+                xtrans(1, q - 1, 0)
+                xtrans(1, q - 1, 1)
+            if q == 2:
+                xcopy(1, 1, 0)
+                xcopy(1, 1, 1)
+            for i in (2 * q + 2, 2 * q + 3):
+                if q > 0 and i in COPY_ON_V:
+                    kcopy(i)
             if q % 2 == 0 and q > 0:
                 finish(q // 2 - 1, 0, 8)
             if last:
@@ -350,11 +391,11 @@ def tile_dpfpattention_pb_kernel(tc, x, wv, beta, vo, k_bytes, k_scale, W, out):
                 finish(3, 6, 8)
             else:
                 pass2(q)
-                if q + 2 < NCH:
-                    wcopy(q + 2, 0)
                 if q == 2:
                     xquant(1, 0)
+                if q == 0:
+                    wquant(2)
+                if q >= 2:
+                    kquant(q)
                 dquant(q)
-                if q + 2 < NCH:
-                    wcopy(q + 2, 1)
                 mm2(q)

from contextlib import ExitStack

import concourse.mybir as mybir
from concourse.masks import make_identity

B, N, D, H, DH = 2, 512, 1024, 16, 64
S = 128
FLOPS = 2 * B * N * D * H * DH + 2 * B * H * N * S * DH

F32 = mybir.dt.float32
BF16 = mybir.dt.bfloat16
U32 = mybir.dt.uint32
U8 = mybir.dt.uint8
FP8 = mybir.dt.float8_e4m3fn
FP8X4 = mybir.dt.float8_e4m3fn_x4
MULT = mybir.AluOpType.mult
ADD = mybir.AluOpType.add
SUB = mybir.AluOpType.subtract
COPY = mybir.ActivationFunctionType.Copy

P = 128
PACK = 4
CHUNKS = ((0, 256), (256, 256), (512, 512))
NCH = len(CHUNKS)
C_OF = (0, 0, 1, 1, 2, 2, 2, 2)
PAIRS = B * H // 2
WIDEN_ON_V = (0,)
COPY_ON_V = (0, 1, 2, 3)
COPY_BY_PE = ()
WCOPY_ON_S = ()
XCOPY_ON_V = ()
QUADS = PAIRS // 2


def tile_dpfpattention_pb_kernel(tc, x, wv, beta, vo, k_bytes, k_scale, W, out):
    nc = tc.nc
    with ExitStack() as ctx:
        keep = ctx.enter_context(tc.tile_pool(name="keep", bufs=1))
        work = ctx.enter_context(tc.tile_pool(name="work", bufs=4))
        psx = ctx.enter_context(tc.psum_pool(name="psx", bufs=2))
        psv = ctx.enter_context(tc.psum_pool(name="psv", bufs=3))
        pso = ctx.enter_context(tc.psum_pool(name="pso", bufs=1))
        psb = ctx.enter_context(tc.psum_pool(name="psb", bufs=1))

        ident = keep.tile([P, P], F32, name="ident")
        identb = keep.tile([P, P], BF16, name="identb")
        brow = keep.tile([P, N], BF16, name="brow")
        pick = keep.tile([P, B * H, 16], BF16, name="pick")
        ksc = keep.tile([P, PACK], F32, name="ksc")
        xc = [[keep.tile([P, 2, 2 * P], U32, align_bytes=64, name="xc%d%d" % (b, u)) for u in range(2)] for b in range(B)]
        xs = [[keep.tile([P, 2, 2 * P], U8, align_bytes=64, name="xs%d%d" % (b, u)) for u in range(2)] for b in range(B)]
        wc = [keep.tile([P, 2, n], U32, align_bytes=64, name="wc%d" % c0) for c0, n in CHUNKS]
        ws = [keep.tile([P, 2, n], U8, align_bytes=64, name="ws%d" % c0) for c0, n in CHUNKS]
        kc = [keep.tile([P, 4 * S], U32, align_bytes=64, name="kc%d" % i) for i in range(QUADS)]
        ks = [keep.tile([P, 4 * S], U8, align_bytes=64, name="ks%d" % i) for i in range(QUADS)]
        dc = [keep.tile([P, 4 * DH], U32, align_bytes=64, name="dc%d" % i) for i in range(QUADS)]
        ds = [keep.tile([P, 4 * DH], U8, align_bytes=64, name="ds%d" % i) for i in range(QUADS)]
        kb = [keep.tile([P, 4, PACK * S], U8, name="kb%d" % q) for q in range(8)]
        vs = [keep.tile([P, 4, PACK, DH], BF16, name="vs%d" % q) for q in range(8)]
        wt = [keep.tile([P, 8, DH], BF16, name="wt%d" % q) for q in range(4)]
        ot = [keep.tile([P, 8, DH], F32, name="ot%d" % q) for q in range(4)]
        xr = [[keep.tile([P, 2, D], BF16, name="xr%d%d" % (b, u)) for u in range(2)] for b in range(B)]
        wr = [keep.tile([P, 2, PACK, n], BF16, name="wr%d" % c0) for c0, n in CHUNKS]
        wg = [keep.tile([P, 2, n, PACK], BF16, align_bytes=64, name="wg%d" % c0) for c0, n in CHUNKS]
        bp = [psb.tile([P, PACK, H * 16], BF16, name="bp%d" % b) for b in range(B)]

        make_identity(nc, identb[:])
        nc.gpsimd.memset(brow[:], 0.0)
        make_identity(nc, ident[:])
        nc.vector.tensor_copy(out=pick[:], in_=identb[:, 0 : B * H].unsqueeze(2).to_broadcast([P, B * H, 16]))

        def load_k(q):
            b, h0 = q // 4, 4 * (q % 4)
            nc.sync.dma_start(
                out=kb[q][:],
                in_=k_bytes[b, h0 : h0 + 4].rearrange("h (p t) s -> p h (t s)", t=PACK),
            )

        def load_vo(q):
            b, h0 = q // 4, 4 * (q % 4)
            nc.sync.dma_start(
                out=vs[q][:].rearrange("p h t d -> p h (t d)"),
                in_=vo[b, h0 : h0 + 4].rearrange("h (p t) d -> p h (t d)", t=PACK),
            )

        def load_x(b, h):
            nc.sync.dma_start(
                out=xr[b][h][:],
                in_=x[b].rearrange("(m t) k -> m t k", t=PACK)[:, 2 * h : 2 * h + 2, :],
            )

        def load_wv(c):
            c0, n = CHUNKS[c]
            for g in range(2):
                nc.sync.dma_start(
                    out=wr[c][:, g],
                    in_=wv.rearrange("(g p j) w -> g p j w", g=2, j=PACK)[g][:, :, c0 : c0 + n],
                )

        def load_w(q):
            b, h0 = q // 2, 8 * (q % 2)
            nc.sync.dma_start(out=wt[q][:], in_=W[b, h0 : h0 + 8].rearrange("h s d -> s h d"))

        nc.sync.dma_start(out=ksc[:], in_=k_scale.rearrange("a c (p t) e -> p (a c t e)", t=PACK))
        load_k(0)
        load_k(1)
        load_x(0, 0)
        load_x(0, 1)
        load_wv(0)
        nc.sync.dma_start(out=brow[0 : B * H, :], in_=beta.rearrange("b h n -> (b h) n"))
        load_k(2)
        load_vo(0)
        load_wv(1)
        load_vo(1)
        load_k(3)
        load_wv(2)
        load_k(4)
        load_vo(2)
        load_x(1, 0)
        load_k(5)
        load_x(1, 1)
        load_vo(3)
        load_k(6)
        load_w(0)
        load_vo(4)
        load_k(7)
        load_vo(5)
        load_w(1)
        load_vo(6)
        load_vo(7)
        load_w(2)
        load_w(3)

        kw_t = {}
        kg_t = {}

        def widen(i):
            kw = work.tile([P, 2, PACK, S], BF16, name="kw", bufs=8)
            kw_t[i] = kw
            for h in range(2):
                src = kb[i // 2]
                for t in range(PACK):
                    sv = src[:, 2 * (i % 2) + h, S * t : S * (t + 1)].bitcast(FP8)
                    if i in WIDEN_ON_V:
                        nc.vector.tensor_scalar(
                            out=kw[:, h, t, :], in0=sv, scalar1=ksc[:, t : t + 1], scalar2=None, op0=MULT
                        )
                    else:
                        nc.scalar.activation(out=kw[:, h, t, :], in_=sv, func=COPY, scale=ksc[:, t : t + 1])

        def kcopy(i):
            if i // 2 not in kg_t:
                kg_t[i // 2] = work.tile([P, 4, S, PACK], BF16, align_bytes=64, name="kg", bufs=6)
            dst = kg_t[i // 2][:, 2 * (i % 2) : 2 * (i % 2) + 2]
            if i in COPY_BY_PE:
                nc.scalar.copy(out=dst, in_=kp_t[i][:])
                return
            dst = dst.rearrange("p h (c i) t -> p h c t i", i=4)
            src = kw_t[i][:].rearrange("p h t (c i) -> p h c t i", i=4)
            if i in COPY_ON_V:
                nc.vector.tensor_copy(out=dst, in_=src)
            else:
                nc.scalar.copy(out=dst, in_=src)

        kp_t = {}

        def kturn(i):
            kp = psx.tile([P, 2, S, PACK], BF16, name="xt")
            kp_t[i] = kp
            for h in range(2):
                nc.tensor.matmul(
                    kp[:, h], lhsT=identb[:], rhs=kw_t[i][:, h].rearrange("p t s -> p s t"), start=True, stop=True
                )

        def kquant(q, a=0, e=4):
            nc.vector.quantize_mx(
                out=kc[q][:, S * a : S * e].bitcast(FP8X4),
                scales=ks[q][:, S * a : S * e],
                in_=kg_t[q][:, a:e].rearrange("p h s t -> p (h s t)"),
            )

        xg_t = {}
        xt_t = {}

        def xtrans(b, h, g):
            xt = psx.tile([P, 2, 2, P], F32, name="xt")
            xt_t[(b, h, g)] = xt
            for tt in range(2):
                words = xr[b][h][:, tt, 512 * g : 512 * (g + 1)].bitcast(F32)
                for u in range(2):
                    nc.tensor.transpose(xt[:, tt, u, :], words[:, u::2], ident[:])

        def xcopy(b, h, g):
            if g == 0:
                xg_t[(b, h)] = work.tile([P, N * PACK], BF16, align_bytes=64, name="xg", bufs=2)
            copy = nc.vector.tensor_copy if (b, h, g) in XCOPY_ON_V else nc.scalar.copy
            copy(
                out=xg_t[(b, h)][:, 1024 * g : 1024 * (g + 1)]
                .bitcast(F32)
                .rearrange("p (t m u) -> p t m u", t=2, u=2),
                in_=xt_t[(b, h, g)][:].rearrange("p t u m -> p t m u"),
            )

        def xquant(b, h):
            nc.vector.quantize_mx(
                out=xc[b][h][:].rearrange("p g n -> p (g n)").bitcast(FP8X4),
                scales=xs[b][h][:].rearrange("p g n -> p (g n)"),
                in_=xg_t[(b, h)][:],
            )

        def wcopy(c, g):
            dst = wg[c][:, g].rearrange("p (c i) j -> p c j i", i=4)
            src = wr[c][:, g].rearrange("p j (c i) -> p c j i", i=4)
            if (c, g) in WCOPY_ON_S:
                nc.scalar.copy(out=dst, in_=src)
            else:
                nc.vector.tensor_copy(out=dst, in_=src)

        def wquant(c):
            nc.vector.quantize_mx(
                out=wc[c][:].rearrange("p g w -> p (g w)").bitcast(FP8X4),
                scales=ws[c][:].rearrange("p g w -> p (g w)"),
                in_=wg[c][:].rearrange("p g w j -> p (g w j)"),
            )

        v_t = {}

        def mm1(i):
            b, j = i // 8, i % 8
            c = C_OF[j]
            o = 128 * j - CHUNKS[c][0]
            v = psv.tile([P, PACK, P], F32, name="v")
            v_t[i] = v
            for t in range(PACK):
                for g in range(2):
                    nc.tensor.matmul_mx(
                        out=v[:, t, :],
                        lhsT=xc[b][t // 2][:, g, P * (t % 2) : P * (t % 2 + 1)].bitcast(FP8X4),
                        lhsT_scale=xs[b][t // 2][:, g, P * (t % 2) : P * (t % 2 + 1)],
                        rhs=wc[c][:, g, o : o + P].bitcast(FP8X4),
                        rhs_scale=ws[c][:, g, o : o + P],
                        start=(g == 0),
                        stop=(g == 1),
                    )

        tm_t = {}
        dg_t = {}

        def pass1(i):
            if i % 2 == 0:
                tm_t[i // 2] = work.tile([P, PACK, 4 * DH], F32, name="tm", bufs=4)
            h0 = 2 * (i % 2)
            nc.vector.tensor_tensor(
                out=tm_t[i // 2][:, :, DH * h0 : DH * (h0 + 2)].rearrange("p t (h d) -> p t h d", h=2),
                in0=v_t[i][:].rearrange("p t (h d) -> p t h d", h=2),
                in1=vs[i // 2][:, h0 : h0 + 2].rearrange("p h t d -> p t h d"),
                op=SUB,
            )

        def pass2(q, a=0, e=4):
            if a == 0:
                dg_t[q] = work.tile([P, 4, DH, PACK], BF16, align_bytes=64, name="dg", bufs=4)
            n = (e - a) * 16
            nc.vector.tensor_tensor(
                out=dg_t[q][:, a:e].rearrange("p h (c i) t -> p (h c) t i", i=4),
                in0=tm_t[q][:, :, DH * a : DH * e].rearrange("p t (c i) -> p c t i", i=4),
                in1=bp[q // 4][:, :, 16 * (4 * (q % 4) + a) : 16 * (4 * (q % 4) + e)]
                .rearrange("p t c -> p c t")
                .unsqueeze(3)
                .to_broadcast([P, n, PACK, 4]),
                op=MULT,
            )

        def dquant(q, a=0, e=4):
            nc.vector.quantize_mx(
                out=dc[q][:, DH * a : DH * e].bitcast(FP8X4),
                scales=ds[q][:, DH * a : DH * e],
                in_=dg_t[q][:, a:e].rearrange("p h d t -> p (h d t)"),
            )

        o_t = {}

        def mm2(q, a=0, e=4):
            if q % 2 == 0 and a == 0:
                o_t[q // 2] = pso.tile([P, 8, DH], F32, name="o")
            for h in range(a, e):
                nc.tensor.matmul_mx(
                    out=o_t[q // 2][:, 4 * (q % 2) + h, :],
                    lhsT=kc[q][:, S * h : S * (h + 1)].bitcast(FP8X4),
                    lhsT_scale=ks[q][:, S * h : S * (h + 1)],
                    rhs=dc[q][:, DH * h : DH * (h + 1)].bitcast(FP8X4),
                    rhs_scale=ds[q][:, DH * h : DH * (h + 1)],
                    start=True,
                    stop=True,
                )

        def finish(q, a, e):
            nc.vector.tensor_tensor(out=ot[q][:, a:e, :], in0=o_t[q][:, a:e, :], in1=wt[q][:, a:e, :], op=ADD)
            b, h0 = q // 2, 8 * (q % 2)
            nc.sync.dma_start(
                out=out[b, h0 + a : h0 + e].rearrange("h s d -> s h d"), in_=ot[q][:, a:e, :]
            )

        def bload(b):
            for t in range(PACK):
                nc.tensor.matmul(
                    bp[b][:, t],
                    lhsT=brow[:, t::PACK],
                    rhs=pick[:, H * b : H * (b + 1)].rearrange("p h c -> p (h c)"),
                    start=True,
                    stop=True,
                )

        widen(0)
        widen(1)
        kcopy(0)
        widen(2)
        kcopy(1)
        widen(3)
        kquant(0)
        kcopy(2)
        kcopy(3)
        xtrans(0, 0, 0)
        xtrans(0, 0, 1)
        xcopy(0, 0, 0)
        xcopy(0, 0, 1)
        kquant(1)
        wcopy(0, 0)
        xtrans(0, 1, 0)
        xtrans(0, 1, 1)
        xcopy(0, 1, 0)
        xcopy(0, 1, 1)
        wcopy(0, 1)
        xquant(0, 0)
        wquant(0)
        bload(0)
        xquant(0, 1)
        mm1(0)
        mm1(1)
        widen(4)
        wcopy(1, 0)
        widen(5)
        wcopy(1, 1)
        for q in range(QUADS):
            last = q == QUADS - 1
            if q == 2:
                bload(1)
                xcopy(1, 0, 0)
                xcopy(1, 0, 1)
            for i in (2 * q + 4, 2 * q + 5):
                if i in COPY_BY_PE:
                    kturn(i)
                if i + 2 < PAIRS:
                    widen(i + 2)
                if i < PAIRS and i not in COPY_ON_V:
                    kcopy(i)
            pass1(2 * q)
            if q == 0:
                wquant(1)
                wcopy(2, 0)
            if q == 3:
                xquant(1, 1)
            if not last:
                mm1(2 * q + 2)
            pass1(2 * q + 1)
            if q == 0:
                wcopy(2, 1)
            if not last:
                mm1(2 * q + 3)
            if q in (1, 2):
                xtrans(1, q - 1, 0)
                xtrans(1, q - 1, 1)
            if q == 2:
                xcopy(1, 1, 0)
                xcopy(1, 1, 1)
            for i in (2 * q + 2, 2 * q + 3):
                if q > 0 and i in COPY_ON_V:
                    kcopy(i)
            if q % 2 == 0 and q > 0:
                finish(q // 2 - 1, 0, 8)
            if last:
                pass2(q, 0, 2)
                kquant(q)
                pass2(q, 2, 4)
                finish(3, 0, 4)
                dquant(q, 0, 2)
                dquant(q, 2, 4)
                mm2(q, 0, 2)
                mm2(q, 2, 4)
                finish(3, 4, 6)
                finish(3, 6, 8)
            else:
                pass2(q)
                if q == 2:
                    xquant(1, 0)
                if q == 0:
                    wquant(2)
                if q >= 2:
                    kquant(q)
                dquant(q)
                mm2(q)
